import numpy as np
import ml_dtypes


def mxq(x, axis, fmt="e4m3"):
    dtype, down = {"e4m3": (ml_dtypes.float8_e4m3fn, 7), "e5m2": (ml_dtypes.float8_e5m2, 14)}[fmt]
    v = np.moveaxis(np.asarray(x, np.float32).astype(ml_dtypes.bfloat16).astype(np.float64), axis, -1)
    blocks = v.reshape(v.shape[:-1] + (-1, 32))
    amax = np.abs(blocks).max(-1, keepdims=True)
    byte = np.maximum(np.where(amax > 0, np.frexp(amax)[1] - 1 + 127, 0) - down, 1)
    scale = np.exp2(byte - 127.0)
    codes = (blocks / scale).astype(np.float32).astype(dtype).astype(np.float64)
    return np.moveaxis((codes * scale).reshape(v.shape), -1, axis)


WIDE = False


def mx_kscale(k):
    if not WIDE:
        return np.ones(k)
    levels = np.array([10, -10, 5, -5, 0])
    a = np.random.permutation(np.resize(levels, k // 512 * 4)).reshape(k // 512, 4)
    idx = np.arange(k)
    return np.exp2(a[idx // 512, idx % 128 // 32])


BF16 = ml_dtypes.bfloat16


def bf(x):
    return np.asarray(x, np.float32).astype(BF16)


def f64(x):
    return np.asarray(x).astype(np.float64)


M, K, N = 4096, 512, 1024


def ternary_quantize(w):
    alpha = np.mean(np.abs(w))
    threshold = 0.7 * alpha
    w_ternary = np.where(np.abs(w) < threshold, np.zeros_like(w), np.sign(w))
    return alpha * w_ternary


def setup_inputs():
    s = mx_kscale(K)
    c = 1.0 / (np.mean(1.0 / s) * np.min(s))
    return {"x": bf(np.random.standard_normal((M, K)) * s),
            "w": bf(np.random.uniform(-1.0, 1.0, (K, N)) * 4.5 / np.sqrt(K) * c / s[:, None]),
            "b": bf(np.random.standard_normal(N) * 0.5)}


def reference(x, w, b):
    wt = ternary_quantize(f64(w))
    return (mxq(f64(x), 1, "e4m3") @ mxq(wt, 0, "e4m3")) + f64(b)

@@ -1,0 +1,168 @@
+from contextlib import ExitStack
+
+import concourse.mybir as mybir
+from concourse.masks import make_identity
+
+F32 = mybir.dt.float32
+BF16 = mybir.dt.bfloat16
+I32 = mybir.dt.int32
+U32 = mybir.dt.uint32
+U8 = mybir.dt.uint8
+FP8X4 = mybir.dt.float8_e4m3fn_x4
+ALU = mybir.AluOpType
+AX = mybir.AxisListType
+
+M, K, N = 4096, 512, 1024
+P = 128
+T = M // P
+HALF = 512
+CH = 4
+NCH = T // CH
+FLOPS = 2 * M * K * N
+COUNT = K * N
+S_BANKS = (2, 4, 7, 9, 11, 13, 15)
+
+
+def tile_ternarydense_t_kernel(tc, x, w, b, out):
+    nc = tc.nc
+    with ExitStack() as ctx:
+        const = ctx.enter_context(tc.tile_pool(name="const", bufs=1))
+        xin = ctx.enter_context(tc.tile_pool(name="xin", bufs=NCH))
+        grp = ctx.enter_context(tc.tile_pool(name="grp", bufs=3))
+        stage = ctx.enter_context(tc.tile_pool(name="stage", bufs=12))
+        ps_t = ctx.enter_context(tc.psum_pool(name="ps_t", bufs=2))
+        ps_o = ctx.enter_context(tc.psum_pool(name="ps_o", bufs=5))
+        ps_m = ctx.enter_context(tc.psum_pool(name="ps_m", bufs=1))
+
+        xv = x.rearrange("(p t) k -> p t k", t=T)
+        ov = out.rearrange("(p t) n -> p t n", t=T)
+
+        w_raw = const.tile([P, 4 * N], BF16, name="w_raw")
+        for u in range(2):
+            nc.sync.dma_start(
+                out=w_raw[:, u * 2 * N : (u + 1) * 2 * N].rearrange("p (e n) -> p e n", e=2),
+                in_=w[u * 256 : (u + 1) * 256, :].rearrange("(q e) n -> q e n", e=2),
+            )
+        brow = const.tile([P, N], BF16, name="brow")
+        nc.vector.memset(brow[:], 0.0)
+        nc.scalar.dma_start(out=brow[0:1, :], in_=b.unsqueeze(0))
+        x_raw = []
+        for c in range(NCH):
+            xr = xin.tile([P, CH * K], BF16, name="xr")
+            nc.sync.dma_start(
+                out=xr[:].rearrange("p (t k) -> p t k", t=CH),
+                in_=xv[:, c * CH : (c + 1) * CH, :],
+            )
+            x_raw.append(xr)
+
+        ones = const.tile([P, P], BF16, name="ones")
+        nc.vector.memset(ones[:], 1.0)
+        ident = const.tile([P, P], F32, name="ident")
+        make_identity(nc, ident[:])
+        cst = const.tile([P, 4], F32, name="cst")
+        nc.gpsimd.memset(cst[:, 0:1], 0.7 / COUNT)
+        nc.gpsimd.memset(cst[:, 1:2], 1.0 / COUNT)
+        nc.gpsimd.memset(cst[:, 2:3], -0.7 / COUNT)
+        nc.gpsimd.memset(cst[:, 3:4], -1.0 / COUNT)
+
+        b_bc = const.tile([P, N], F32, name="b_bc")
+        for h in range(2):
+            pb = ps_m.tile([P, HALF], F32, name="pb", tag="misc")
+            nc.tensor.matmul(pb[:], lhsT=ones[:], rhs=brow[:, h * HALF : (h + 1) * HALF], start=True, stop=True)
+            nc.scalar.copy(out=b_bc[:, h * HALF : (h + 1) * HALF], in_=pb[:])
+
+        aw = const.tile([P, 4 * N], BF16, name="aw")
+        for u in range(2):
+            sl = slice(u * 2 * N, (u + 1) * 2 * N)
+            nc.vector.tensor_single_scalar(
+                out=aw[:, sl].bitcast(I32), in_=w_raw[:, sl].bitcast(I32), scalar=0x7FFF7FFF, op=ALU.bitwise_and
+            )
+        psum_s = ps_m.tile([P, P], F32, name="psum_s", tag="misc")
+        nsum = 4 * N // P
+        for c in range(nsum):
+            nc.tensor.matmul(psum_s[:], lhsT=ones[:], rhs=aw[:, c * P : (c + 1) * P], start=(c == 0), stop=(c == nsum - 1))
+
+        wg = const.tile([P, 4 * N], BF16, name="wg", align_bytes=64)
+        w_tn = w_raw[:].rearrange("p (t n) -> p t n", t=4)
+        for h in range(2):
+            dst = wg[:, h * 4 * HALF : (h + 1) * 4 * HALF].rearrange("p (c i t) -> p c t i", i=4, t=4)
+            src = w_tn[:, :, h * HALF : (h + 1) * HALF].rearrange("p t (c i) -> p c t i", i=4)
+            if h == 0:
+                nc.vector.tensor_copy(out=dst, in_=src)
+            else:
+                nc.scalar.copy(out=dst, in_=src)
+
+        tot = const.tile([P, 1], F32, name="tot")
+        nc.vector.tensor_reduce(out=tot[:], in_=psum_s[:], axis=AX.X, op=ALU.add)
+        sc = const.tile([P, 4], F32, name="sc")
+        nc.vector.tensor_scalar(out=sc[:], in0=cst[:], scalar1=tot[:, 0:1], scalar2=None, op0=ALU.mult)
+
+        x_codes = const.tile([P, T * P], U32, name="x_codes", align_bytes=64)
+        x_scales = const.tile([P, T * P], U8, name="x_scales", align_bytes=64)
+
+        def prepare_x(c):
+            xw = x_raw[c][:].bitcast(F32)
+            g = grp.tile([P, CH * K], BF16, name="g", align_bytes=64)
+            gw = g[:].bitcast(F32)
+            for j in range(CH // 2):
+                xt = ps_t.tile([P, 2, 2, P], F32, name="xt")
+                for r in range(2):
+                    for u in range(2):
+                        col = (2 * j + r) * 256 + u * P
+                        nc.tensor.transpose(xt[:, r, u, :], xw[:, col : col + P], ident[:])
+                nc.scalar.copy(
+                    out=gw[:, j * 512 : (j + 1) * 512].rearrange("p (r m u) -> p r m u", r=2, u=2),
+                    in_=xt[:].rearrange("p r u m -> p r m u"),
+                )
+            cs = slice(c * CH * P, (c + 1) * CH * P)
+            nc.vector.quantize_mx(out=x_codes[:, cs].bitcast(FP8X4), scales=x_scales[:, cs], in_=g[:])
+
+        prepare_x(0)
+
+        t1 = const.tile([P, 4 * N], BF16, name="t1")
+        t2 = const.tile([P, 4 * N], BF16, name="t2")
+        wt = const.tile([P, 4 * N], BF16, name="wt", align_bytes=64)
+        w_codes = const.tile([P, N], U32, name="w_codes", align_bytes=64)
+        w_scales = const.tile([P, N], U8, name="w_scales", align_bytes=64)
+        for h in range(2):
+            sl = slice(h * 4 * HALF, (h + 1) * 4 * HALF)
+            hs = slice(h * HALF, (h + 1) * HALF)
+            nc.vector.tensor_scalar(
+                out=t1[:, sl], in0=wg[:, sl], scalar1=sc[:, 0:1], scalar2=sc[:, 1:2], op0=ALU.is_ge, op1=ALU.mult
+            )
+            nc.vector.tensor_scalar(
+                out=t2[:, sl], in0=wg[:, sl], scalar1=sc[:, 2:3], scalar2=sc[:, 3:4], op0=ALU.is_le, op1=ALU.mult
+            )
+            nc.vector.tensor_tensor(out=wt[:, sl], in0=t1[:, sl], in1=t2[:, sl], op=ALU.add)
+            nc.vector.quantize_mx(out=w_codes[:, hs].bitcast(FP8X4), scales=w_scales[:, hs], in_=wt[:, sl])
+
+        def multiply(c):
+            for j in range(CH // 2):
+                o = stage.tile([P, 2, N], F32, name="o")
+                for r in range(2):
+                    t = c * CH + 2 * j + r
+                    ts = slice(t * P, (t + 1) * P)
+                    for h in range(2):
+                        hs = slice(h * HALF, (h + 1) * HALF)
+                        acc = ps_o.tile([P, HALF], F32, name="acc")
+                        nc.tensor.matmul_mx(
+                            out=acc[:],
+                            lhsT=x_codes[:, ts].bitcast(FP8X4),
+                            lhsT_scale=x_scales[:, ts],
+                            rhs=w_codes[:, hs].bitcast(FP8X4),
+                            rhs_scale=w_scales[:, hs],
+                            start=True,
+                            stop=True,
+                        )
+                        if (2 * t + h) % 16 in S_BANKS:
+                            nc.scalar.copy(out=o[:, r, hs], in_=acc[:])
+                            nc.gpsimd.tensor_tensor(out=o[:, r, hs], in0=o[:, r, hs], in1=b_bc[:, hs], op=ALU.add)
+                        else:
+                            nc.vector.tensor_tensor(out=o[:, r, hs], in0=acc[:], in1=b_bc[:, hs], op=ALU.add)
+                t0 = c * CH + 2 * j
+                nc.sync.dma_start(out=ov[:, t0 : t0 + 2, :], in_=o[:])
+
+        for c in range(NCH):
+            if c + 1 < NCH:
+                prepare_x(c + 1)
+            multiply(c)

@@ -20,7 +20,13 @@ CH = 4
 NCH = T // CH
 FLOPS = 2 * M * K * N
 COUNT = K * N
-S_BANKS = (2, 4, 7, 9, 11, 13, 15)
+NWARM = 7
+GROUPS = (
+    [(0, 1, ((0, 0),)), (1, 1, ((0, 0),)), (2, 2, ((0, 0),))]
+    + [(t, 2, ((0, 0), (1, 0)) if t % 4 == 0 else ((0, 0),)) for t in range(4, 28, 2)]
+    + [(28, 2, ((0, 0),)), (30, 2, ())]
+)
+LEAD = 2
 
 
 def tile_ternarydense_t_kernel(tc, x, w, b, out):
@@ -31,21 +37,33 @@ def tile_ternarydense_t_kernel(tc, x, w, b, out):
         grp = ctx.enter_context(tc.tile_pool(name="grp", bufs=3))
         stage = ctx.enter_context(tc.tile_pool(name="stage", bufs=12))
         ps_t = ctx.enter_context(tc.psum_pool(name="ps_t", bufs=2))
-        ps_o = ctx.enter_context(tc.psum_pool(name="ps_o", bufs=5))
-        ps_m = ctx.enter_context(tc.psum_pool(name="ps_m", bufs=1))
+        ps_o = ctx.enter_context(tc.psum_pool(name="ps_o", bufs=6))
+        ctx.enter_context(tc.manual_schedule())
 
         xv = x.rearrange("(p t) k -> p t k", t=T)
         ov = out.rearrange("(p t) n -> p t n", t=T)
 
+        brow = const.tile([P, N], BF16, name="brow")
+        nc.vector.memset(brow[:], 0.0)
+        ones = const.tile([P, P], BF16, name="ones")
+        nc.vector.memset(ones[:], 1.0)
+        zeros = const.tile([P, HALF], BF16, name="zeros")
+        nc.vector.memset(zeros[:], 0.0)
+        ident = const.tile([P, P], F32, name="ident")
+        make_identity(nc, ident[:])
+        cst = const.tile([P, 4], F32, name="cst")
+        nc.gpsimd.memset(cst[:, 0:1], 0.7 / COUNT)
+        nc.gpsimd.memset(cst[:, 1:2], 1.0 / COUNT)
+        nc.gpsimd.memset(cst[:, 2:3], -0.7 / COUNT)
+        nc.gpsimd.memset(cst[:, 3:4], -1.0 / COUNT)
+
+        nc.sync.dma_start(out=brow[0:1, :], in_=b.unsqueeze(0))
         w_raw = const.tile([P, 4 * N], BF16, name="w_raw")
         for u in range(2):
             nc.sync.dma_start(
                 out=w_raw[:, u * 2 * N : (u + 1) * 2 * N].rearrange("p (e n) -> p e n", e=2),
                 in_=w[u * 256 : (u + 1) * 256, :].rearrange("(q e) n -> q e n", e=2),
             )
-        brow = const.tile([P, N], BF16, name="brow")
-        nc.vector.memset(brow[:], 0.0)
-        nc.scalar.dma_start(out=brow[0:1, :], in_=b.unsqueeze(0))
         x_raw = []
         for c in range(NCH):
             xr = xin.tile([P, CH * K], BF16, name="xr")
@@ -55,32 +73,22 @@ def tile_ternarydense_t_kernel(tc, x, w, b, out):
             )
             x_raw.append(xr)
 
-        ones = const.tile([P, P], BF16, name="ones")
-        nc.vector.memset(ones[:], 1.0)
-        ident = const.tile([P, P], F32, name="ident")
-        make_identity(nc, ident[:])
-        cst = const.tile([P, 4], F32, name="cst")
-        nc.gpsimd.memset(cst[:, 0:1], 0.7 / COUNT)
-        nc.gpsimd.memset(cst[:, 1:2], 1.0 / COUNT)
-        nc.gpsimd.memset(cst[:, 2:3], -0.7 / COUNT)
-        nc.gpsimd.memset(cst[:, 3:4], -1.0 / COUNT)
-
-        b_bc = const.tile([P, N], F32, name="b_bc")
-        for h in range(2):
-            pb = ps_m.tile([P, HALF], F32, name="pb", tag="misc")
-            nc.tensor.matmul(pb[:], lhsT=ones[:], rhs=brow[:, h * HALF : (h + 1) * HALF], start=True, stop=True)
-            nc.scalar.copy(out=b_bc[:, h * HALF : (h + 1) * HALF], in_=pb[:])
+        warm = ps_o.tile([P, HALF], F32, name="warm", tag="acc")
+        for i in range(NWARM):
+            nc.tensor.matmul(warm[:], lhsT=ones[:], rhs=zeros[:], start=True, stop=True)
 
         aw = const.tile([P, 4 * N], BF16, name="aw")
-        for u in range(2):
-            sl = slice(u * 2 * N, (u + 1) * 2 * N)
+        psum_s = ps_o.tile([P, P], F32, name="psum_s", tag="acc")
+        nsum = 4 * N // P
+        for q in range(4):
+            sl = slice(q * N, (q + 1) * N)
             nc.vector.tensor_single_scalar(
                 out=aw[:, sl].bitcast(I32), in_=w_raw[:, sl].bitcast(I32), scalar=0x7FFF7FFF, op=ALU.bitwise_and
             )
-        psum_s = ps_m.tile([P, P], F32, name="psum_s", tag="misc")
-        nsum = 4 * N // P
-        for c in range(nsum):
-            nc.tensor.matmul(psum_s[:], lhsT=ones[:], rhs=aw[:, c * P : (c + 1) * P], start=(c == 0), stop=(c == nsum - 1))
+            for c in range(q * 8, q * 8 + 8):
+                nc.tensor.matmul(
+                    psum_s[:], lhsT=ones[:], rhs=aw[:, c * P : (c + 1) * P], start=(c == 0), stop=(c == nsum - 1)
+                )
 
         wg = const.tile([P, 4 * N], BF16, name="wg", align_bytes=64)
         w_tn = w_raw[:].rearrange("p (t n) -> p t n", t=4)
@@ -92,15 +100,11 @@ def tile_ternarydense_t_kernel(tc, x, w, b, out):
             else:
                 nc.scalar.copy(out=dst, in_=src)
 
-        tot = const.tile([P, 1], F32, name="tot")
-        nc.vector.tensor_reduce(out=tot[:], in_=psum_s[:], axis=AX.X, op=ALU.add)
-        sc = const.tile([P, 4], F32, name="sc")
-        nc.vector.tensor_scalar(out=sc[:], in0=cst[:], scalar1=tot[:, 0:1], scalar2=None, op0=ALU.mult)
-
         x_codes = const.tile([P, T * P], U32, name="x_codes", align_bytes=64)
         x_scales = const.tile([P, T * P], U8, name="x_scales", align_bytes=64)
+        groups = {}
 
-        def prepare_x(c):
+        def turn_x(c):
             xw = x_raw[c][:].bitcast(F32)
             g = grp.tile([P, CH * K], BF16, name="g", align_bytes=64)
             gw = g[:].bitcast(F32)
@@ -114,11 +118,28 @@ def tile_ternarydense_t_kernel(tc, x, w, b, out):
                     out=gw[:, j * 512 : (j + 1) * 512].rearrange("p (r m u) -> p r m u", r=2, u=2),
                     in_=xt[:].rearrange("p r u m -> p r m u"),
                 )
+            groups[c] = g
+
+        def quantise_x(c):
             cs = slice(c * CH * P, (c + 1) * CH * P)
-            nc.vector.quantize_mx(out=x_codes[:, cs].bitcast(FP8X4), scales=x_scales[:, cs], in_=g[:])
+            nc.vector.quantize_mx(out=x_codes[:, cs].bitcast(FP8X4), scales=x_scales[:, cs], in_=groups[c][:])
 
-        prepare_x(0)
+        b_bc = const.tile([P, N], F32, name="b_bc")
+        pbs = []
+        for h in range(2):
+            pb = ps_o.tile([P, HALF], F32, name="pb", tag="acc")
+            nc.tensor.matmul(pb[:], lhsT=ones[:], rhs=brow[:, h * HALF : (h + 1) * HALF], start=True, stop=True)
+            pbs.append(pb)
+        turn_x(0)
+        for h in range(2):
+            nc.scalar.copy(out=b_bc[:, h * HALF : (h + 1) * HALF], in_=pbs[h][:])
+        turn_x(1)
+        turn_x(2)
 
+        tot = const.tile([P, 1], F32, name="tot")
+        nc.vector.tensor_reduce(out=tot[:], in_=psum_s[:], axis=AX.X, op=ALU.add)
+        sc = const.tile([P, 4], F32, name="sc")
+        nc.vector.tensor_scalar(out=sc[:], in0=cst[:], scalar1=tot[:, 0:1], scalar2=None, op0=ALU.mult)
         t1 = const.tile([P, 4 * N], BF16, name="t1")
         t2 = const.tile([P, 4 * N], BF16, name="t2")
         wt = const.tile([P, 4 * N], BF16, name="wt", align_bytes=64)
@@ -134,35 +155,51 @@ def tile_ternarydense_t_kernel(tc, x, w, b, out):
                 out=t2[:, sl], in0=wg[:, sl], scalar1=sc[:, 2:3], scalar2=sc[:, 3:4], op0=ALU.is_le, op1=ALU.mult
             )
             nc.vector.tensor_tensor(out=wt[:, sl], in0=t1[:, sl], in1=t2[:, sl], op=ALU.add)
+            quantise_x(h)
             nc.vector.quantize_mx(out=w_codes[:, hs].bitcast(FP8X4), scales=w_scales[:, hs], in_=wt[:, sl])
 
-        def multiply(c):
-            for j in range(CH // 2):
-                o = stage.tile([P, 2, N], F32, name="o")
-                for r in range(2):
-                    t = c * CH + 2 * j + r
-                    ts = slice(t * P, (t + 1) * P)
-                    for h in range(2):
-                        hs = slice(h * HALF, (h + 1) * HALF)
-                        acc = ps_o.tile([P, HALF], F32, name="acc")
-                        nc.tensor.matmul_mx(
-                            out=acc[:],
-                            lhsT=x_codes[:, ts].bitcast(FP8X4),
-                            lhsT_scale=x_scales[:, ts],
-                            rhs=w_codes[:, hs].bitcast(FP8X4),
-                            rhs_scale=w_scales[:, hs],
-                            start=True,
-                            stop=True,
-                        )
-                        if (2 * t + h) % 16 in S_BANKS:
-                            nc.scalar.copy(out=o[:, r, hs], in_=acc[:])
-                            nc.gpsimd.tensor_tensor(out=o[:, r, hs], in0=o[:, r, hs], in1=b_bc[:, hs], op=ALU.add)
-                        else:
-                            nc.vector.tensor_tensor(out=o[:, r, hs], in0=acc[:], in1=b_bc[:, hs], op=ALU.add)
-                t0 = c * CH + 2 * j
-                nc.sync.dma_start(out=ov[:, t0 : t0 + 2, :], in_=o[:])
+        o_tiles = {}
 
-        for c in range(NCH):
-            if c + 1 < NCH:
-                prepare_x(c + 1)
-            multiply(c)
+        def bank(j, t, h, who):
+            t0, nt = GROUPS[j][0], GROUPS[j][1]
+            if j not in o_tiles:
+                o_tiles[j] = stage.tile([P, nt, N], F32, name="o")
+            o = o_tiles[j]
+            ts = slice(t * P, (t + 1) * P)
+            hs = slice(h * HALF, (h + 1) * HALF)
+            acc = ps_o.tile([P, HALF], F32, name="acc")
+            nc.tensor.matmul_mx(
+                out=acc[:],
+                lhsT=x_codes[:, ts].bitcast(FP8X4),
+                lhsT_scale=x_scales[:, ts],
+                rhs=w_codes[:, hs].bitcast(FP8X4),
+                rhs_scale=w_scales[:, hs],
+                start=True,
+                stop=True,
+            )
+            if who == "s":
+                nc.scalar.copy(out=o[:, t - t0, hs], in_=acc[:])
+                nc.gpsimd.tensor_tensor(out=o[:, t - t0, hs], in0=o[:, t - t0, hs], in1=b_bc[:, hs], op=ALU.add)
+            else:
+                nc.vector.tensor_tensor(out=o[:, t - t0, hs], in0=acc[:], in1=b_bc[:, hs], op=ALU.add)
+
+        def banks_of(j, who):
+            t0, nt, s_set = GROUPS[j]
+            for t in range(t0, t0 + nt):
+                for h in range(2):
+                    if ((t - t0, h) in s_set) == (who == "s"):
+                        bank(j, t, h, who)
+
+        for j in range(LEAD):
+            banks_of(j, "s")
+        for j in range(len(GROUPS)):
+            t0, nt, s_set = GROUPS[j]
+            c = t0 // CH
+            if t0 % CH == 0 and c + 2 < NCH:
+                quantise_x(c + 2)
+            if j + LEAD < len(GROUPS):
+                banks_of(j + LEAD, "s")
+            if t0 % CH == 2 and c + 3 < NCH:
+                turn_x(c + 3)
+            banks_of(j, "v")
+            nc.sync.dma_start(out=ov[:, t0 : t0 + nt, :], in_=o_tiles[j][:])

@@ -21,12 +21,22 @@ NCH = T // CH
 FLOPS = 2 * M * K * N
 COUNT = K * N
 NWARM = 7
-GROUPS = (
-    [(0, 1, ((0, 0),)), (1, 1, ((0, 0),)), (2, 2, ((0, 0),))]
-    + [(t, 2, ((0, 0), (1, 0)) if t % 4 == 0 else ((0, 0),)) for t in range(4, 28, 2)]
-    + [(28, 2, ((0, 0),)), (30, 2, ())]
-)
-LEAD = 2
+NWARM2 = 5
+LEAD = 3
+EARLY = 2
+
+
+def build_groups():
+    groups = [(t, 1, ((0, 0),)) for t in range(4)]
+    for t in range(4, T, 2):
+        s_set = ((0, 0), (1, 0)) if t % 4 == 0 else ((0, 0),)
+        if t >= T - 4:
+            s_set = ((0, 0),) if t == T - 4 else ()
+        groups.append((t, 2, s_set))
+    return groups
+
+
+GROUPS = build_groups()
 
 
 def tile_ternarydense_t_kernel(tc, x, w, b, out):
@@ -34,10 +44,9 @@ def tile_ternarydense_t_kernel(tc, x, w, b, out):
     with ExitStack() as ctx:
         const = ctx.enter_context(tc.tile_pool(name="const", bufs=1))
         xin = ctx.enter_context(tc.tile_pool(name="xin", bufs=NCH))
-        grp = ctx.enter_context(tc.tile_pool(name="grp", bufs=3))
-        stage = ctx.enter_context(tc.tile_pool(name="stage", bufs=12))
-        ps_t = ctx.enter_context(tc.psum_pool(name="ps_t", bufs=2))
-        ps_o = ctx.enter_context(tc.psum_pool(name="ps_o", bufs=6))
+        grp = ctx.enter_context(tc.tile_pool(name="grp", bufs=NCH))
+        stage = ctx.enter_context(tc.tile_pool(name="stage", bufs=9))
+        ps_o = ctx.enter_context(tc.psum_pool(name="ps_o", bufs=8))
         ctx.enter_context(tc.manual_schedule())
 
         xv = x.rearrange("(p t) k -> p t k", t=T)
@@ -57,13 +66,13 @@ def tile_ternarydense_t_kernel(tc, x, w, b, out):
         nc.gpsimd.memset(cst[:, 2:3], -0.7 / COUNT)
         nc.gpsimd.memset(cst[:, 3:4], -1.0 / COUNT)
 
-        nc.sync.dma_start(out=brow[0:1, :], in_=b.unsqueeze(0))
         w_raw = const.tile([P, 4 * N], BF16, name="w_raw")
         for u in range(2):
             nc.sync.dma_start(
                 out=w_raw[:, u * 2 * N : (u + 1) * 2 * N].rearrange("p (e n) -> p e n", e=2),
                 in_=w[u * 256 : (u + 1) * 256, :].rearrange("(q e) n -> q e n", e=2),
             )
+        nc.sync.dma_start(out=brow[0:1, :], in_=b.unsqueeze(0))
         x_raw = []
         for c in range(NCH):
             xr = xin.tile([P, CH * K], BF16, name="xr")
@@ -104,21 +113,21 @@ def tile_ternarydense_t_kernel(tc, x, w, b, out):
         x_scales = const.tile([P, T * P], U8, name="x_scales", align_bytes=64)
         groups = {}
 
-        def turn_x(c):
+        def turn_x(i):
+            c, j = i // 2, i % 2
             xw = x_raw[c][:].bitcast(F32)
-            g = grp.tile([P, CH * K], BF16, name="g", align_bytes=64)
-            gw = g[:].bitcast(F32)
-            for j in range(CH // 2):
-                xt = ps_t.tile([P, 2, 2, P], F32, name="xt")
-                for r in range(2):
-                    for u in range(2):
-                        col = (2 * j + r) * 256 + u * P
-                        nc.tensor.transpose(xt[:, r, u, :], xw[:, col : col + P], ident[:])
-                nc.scalar.copy(
-                    out=gw[:, j * 512 : (j + 1) * 512].rearrange("p (r m u) -> p r m u", r=2, u=2),
-                    in_=xt[:].rearrange("p r u m -> p r m u"),
-                )
-            groups[c] = g
+            if j == 0:
+                groups[c] = grp.tile([P, CH * K], BF16, name="g", align_bytes=64)
+            gw = groups[c][:].bitcast(F32)
+            xt = ps_o.tile([P, 2, 2, P], F32, name="xt", tag="acc")
+            for r in range(2):
+                for u in range(2):
+                    col = (2 * j + r) * 256 + u * P
+                    nc.tensor.transpose(xt[:, r, u, :], xw[:, col : col + P], ident[:])
+            nc.scalar.copy(
+                out=gw[:, j * 512 : (j + 1) * 512].rearrange("p (r m u) -> p r m u", r=2, u=2),
+                in_=xt[:].rearrange("p r u m -> p r m u"),
+            )
 
         def quantise_x(c):
             cs = slice(c * CH * P, (c + 1) * CH * P)
@@ -130,11 +139,13 @@ def tile_ternarydense_t_kernel(tc, x, w, b, out):
             pb = ps_o.tile([P, HALF], F32, name="pb", tag="acc")
             nc.tensor.matmul(pb[:], lhsT=ones[:], rhs=brow[:, h * HALF : (h + 1) * HALF], start=True, stop=True)
             pbs.append(pb)
-        turn_x(0)
+        for i in range(4):
+            turn_x(i)
         for h in range(2):
             nc.scalar.copy(out=b_bc[:, h * HALF : (h + 1) * HALF], in_=pbs[h][:])
-        turn_x(1)
-        turn_x(2)
+
+        for i in range(NWARM2):
+            nc.tensor.matmul(warm[:], lhsT=ones[:], rhs=zeros[:], start=True, stop=True)
 
         tot = const.tile([P, 1], F32, name="tot")
         nc.vector.tensor_reduce(out=tot[:], in_=psum_s[:], axis=AX.X, op=ALU.add)
@@ -145,26 +156,32 @@ def tile_ternarydense_t_kernel(tc, x, w, b, out):
         wt = const.tile([P, 4 * N], BF16, name="wt", align_bytes=64)
         w_codes = const.tile([P, N], U32, name="w_codes", align_bytes=64)
         w_scales = const.tile([P, N], U8, name="w_scales", align_bytes=64)
-        for h in range(2):
+        def w_step(h, i):
             sl = slice(h * 4 * HALF, (h + 1) * 4 * HALF)
             hs = slice(h * HALF, (h + 1) * HALF)
-            nc.vector.tensor_scalar(
-                out=t1[:, sl], in0=wg[:, sl], scalar1=sc[:, 0:1], scalar2=sc[:, 1:2], op0=ALU.is_ge, op1=ALU.mult
-            )
-            nc.vector.tensor_scalar(
-                out=t2[:, sl], in0=wg[:, sl], scalar1=sc[:, 2:3], scalar2=sc[:, 3:4], op0=ALU.is_le, op1=ALU.mult
-            )
-            nc.vector.tensor_tensor(out=wt[:, sl], in0=t1[:, sl], in1=t2[:, sl], op=ALU.add)
-            quantise_x(h)
-            nc.vector.quantize_mx(out=w_codes[:, hs].bitcast(FP8X4), scales=w_scales[:, hs], in_=wt[:, sl])
+            if i == 0:
+                nc.vector.tensor_scalar(
+                    out=t1[:, sl], in0=wg[:, sl], scalar1=sc[:, 0:1], scalar2=sc[:, 1:2], op0=ALU.is_ge, op1=ALU.mult
+                )
+            elif i == 1:
+                nc.vector.tensor_scalar(
+                    out=t2[:, sl], in0=wg[:, sl], scalar1=sc[:, 2:3], scalar2=sc[:, 3:4], op0=ALU.is_le, op1=ALU.mult
+                )
+            elif i == 2:
+                nc.vector.tensor_tensor(out=wt[:, sl], in0=t1[:, sl], in1=t2[:, sl], op=ALU.add)
+            else:
+                nc.vector.quantize_mx(out=w_codes[:, hs].bitcast(FP8X4), scales=w_scales[:, hs], in_=wt[:, sl])
+
+        for i in range(3):
+            w_step(0, i)
+        quantise_x(0)
+        w_step(0, 3)
 
         o_tiles = {}
 
-        def bank(j, t, h, who):
-            t0, nt = GROUPS[j][0], GROUPS[j][1]
-            if j not in o_tiles:
-                o_tiles[j] = stage.tile([P, nt, N], F32, name="o")
-            o = o_tiles[j]
+        accs = {}
+
+        def multiply(j, t, h):
             ts = slice(t * P, (t + 1) * P)
             hs = slice(h * HALF, (h + 1) * HALF)
             acc = ps_o.tile([P, HALF], F32, name="acc")
@@ -177,29 +194,54 @@ def tile_ternarydense_t_kernel(tc, x, w, b, out):
                 start=True,
                 stop=True,
             )
+            accs[(t, h)] = acc
+
+        def leave(j, t, h, who):
+            t0, nt = GROUPS[j][0], GROUPS[j][1]
+            if j not in o_tiles:
+                o_tiles[j] = stage.tile([P, nt, N], F32, name="o")
+            hs = slice(h * HALF, (h + 1) * HALF)
+            dst = o_tiles[j][:, t - t0, hs]
+            acc = accs[(t, h)]
             if who == "s":
-                nc.scalar.copy(out=o[:, t - t0, hs], in_=acc[:])
-                nc.gpsimd.tensor_tensor(out=o[:, t - t0, hs], in0=o[:, t - t0, hs], in1=b_bc[:, hs], op=ALU.add)
+                nc.scalar.copy(out=dst, in_=acc[:])
+                nc.gpsimd.tensor_tensor(out=dst, in0=dst, in1=b_bc[:, hs], op=ALU.add)
             else:
-                nc.vector.tensor_tensor(out=o[:, t - t0, hs], in0=acc[:], in1=b_bc[:, hs], op=ALU.add)
+                nc.vector.tensor_tensor(out=dst, in0=acc[:], in1=b_bc[:, hs], op=ALU.add)
 
         def banks_of(j, who):
             t0, nt, s_set = GROUPS[j]
-            for t in range(t0, t0 + nt):
-                for h in range(2):
-                    if ((t - t0, h) in s_set) == (who == "s"):
-                        bank(j, t, h, who)
+            return [(t, h) for t in range(t0, t0 + nt) for h in range(2) if ((t - t0, h) in s_set) == (who == "s")]
 
-        for j in range(LEAD):
-            banks_of(j, "s")
+        def s_banks(j):
+            for t, h in banks_of(j, "s"):
+                multiply(j, t, h)
+                leave(j, t, h, "s")
+
+        for j in range(4):
+            s_banks(j)
+            if j < EARLY:
+                turn_x(j + 4)
+        for i in range(3):
+            w_step(1, i)
+        quantise_x(1)
+        w_step(1, 3)
+        for t, h in banks_of(0, "v"):
+            multiply(0, t, h)
+        s_done = 4
         for j in range(len(GROUPS)):
             t0, nt, s_set = GROUPS[j]
             c = t0 // CH
-            if t0 % CH == 0 and c + 2 < NCH:
+            for t, h in banks_of(j, "v"):
+                leave(j, t, h, "v")
+            if (t0 == 3 or (t0 >= CH and t0 % CH == 0)) and c + 2 < NCH:
                 quantise_x(c + 2)
-            if j + LEAD < len(GROUPS):
-                banks_of(j + LEAD, "s")
-            if t0 % CH == 2 and c + 3 < NCH:
-                turn_x(c + 3)
-            banks_of(j, "v")
+            if j + 1 < len(GROUPS):
+                for t, h in banks_of(j + 1, "v"):
+                    multiply(j + 1, t, h)
+            while s_done < len(GROUPS) and s_done <= max(j + LEAD, 5) and (s_done < 6 or j >= 3):
+                s_banks(s_done)
+                s_done += 1
+            if j + 4 + EARLY < 2 * NCH:
+                turn_x(j + 4 + EARLY)
             nc.sync.dma_start(out=ov[:, t0 : t0 + nt, :], in_=o_tiles[j][:])

@@ -20,14 +20,15 @@ CH = 4
 NCH = T // CH
 FLOPS = 2 * M * K * N
 COUNT = K * N
-NWARM = 7
-NWARM2 = 5
+NWARM = 3
+NWARM2 = 0
+SUMW = 256
 LEAD = 3
 EARLY = 2
 
 
 def build_groups():
-    groups = [(t, 1, ((0, 0),)) for t in range(4)]
+    groups = [(t, 1, ((0, 0),) if t % 2 == 1 else ()) for t in range(4)]
     for t in range(4, T, 2):
         s_set = ((0, 0), (1, 0)) if t % 4 == 0 else ((0, 0),)
         if t >= T - 4:
@@ -52,12 +53,12 @@ def tile_ternarydense_t_kernel(tc, x, w, b, out):
         xv = x.rearrange("(p t) k -> p t k", t=T)
         ov = out.rearrange("(p t) n -> p t n", t=T)
 
-        brow = const.tile([P, N], BF16, name="brow")
-        nc.vector.memset(brow[:], 0.0)
         ones = const.tile([P, P], BF16, name="ones")
         nc.vector.memset(ones[:], 1.0)
         zeros = const.tile([P, HALF], BF16, name="zeros")
-        nc.vector.memset(zeros[:], 0.0)
+        nc.vector.memset(zeros[:].bitcast(I32), 0)
+        brow = const.tile([P, N], BF16, name="brow")
+        nc.gpsimd.memset(brow[:], 0.0)
         ident = const.tile([P, P], F32, name="ident")
         make_identity(nc, ident[:])
         cst = const.tile([P, 4], F32, name="cst")
@@ -87,16 +88,16 @@ def tile_ternarydense_t_kernel(tc, x, w, b, out):
             nc.tensor.matmul(warm[:], lhsT=ones[:], rhs=zeros[:], start=True, stop=True)
 
         aw = const.tile([P, 4 * N], BF16, name="aw")
-        psum_s = ps_o.tile([P, P], F32, name="psum_s", tag="acc")
-        nsum = 4 * N // P
+        psum_s = ps_o.tile([P, SUMW], F32, name="psum_s", tag="acc")
+        nsum = 4 * N // SUMW
         for q in range(4):
             sl = slice(q * N, (q + 1) * N)
             nc.vector.tensor_single_scalar(
                 out=aw[:, sl].bitcast(I32), in_=w_raw[:, sl].bitcast(I32), scalar=0x7FFF7FFF, op=ALU.bitwise_and
             )
-            for c in range(q * 8, q * 8 + 8):
+            for c in range(q * nsum // 4, (q + 1) * nsum // 4):
                 nc.tensor.matmul(
-                    psum_s[:], lhsT=ones[:], rhs=aw[:, c * P : (c + 1) * P], start=(c == 0), stop=(c == nsum - 1)
+                    psum_s[:], lhsT=ones[:], rhs=aw[:, c * SUMW : (c + 1) * SUMW], start=(c == 0), stop=(c == nsum - 1)
                 )
 
         wg = const.tile([P, 4 * N], BF16, name="wg", align_bytes=64)
@@ -222,24 +223,24 @@ def tile_ternarydense_t_kernel(tc, x, w, b, out):
             s_banks(j)
             if j < EARLY:
                 turn_x(j + 4)
-        for i in range(3):
+        multiply(0, 0, 0)
+        for i in range(4):
             w_step(1, i)
-        quantise_x(1)
-        w_step(1, 3)
-        for t, h in banks_of(0, "v"):
-            multiply(0, t, h)
+        multiply(0, 0, 1)
         s_done = 4
         for j in range(len(GROUPS)):
             t0, nt, s_set = GROUPS[j]
             c = t0 // CH
             for t, h in banks_of(j, "v"):
                 leave(j, t, h, "v")
+            if t0 == 1:
+                quantise_x(1)
             if (t0 == 3 or (t0 >= CH and t0 % CH == 0)) and c + 2 < NCH:
                 quantise_x(c + 2)
             if j + 1 < len(GROUPS):
                 for t, h in banks_of(j + 1, "v"):
                     multiply(j + 1, t, h)
-            while s_done < len(GROUPS) and s_done <= max(j + LEAD, 5) and (s_done < 6 or j >= 3):
+            while s_done < len(GROUPS) and s_done <= max(j + LEAD, 5) and j >= (1 if s_done < 6 else 3):
                 s_banks(s_done)
                 s_done += 1
             if j + 4 + EARLY < 2 * NCH:

@@ -21,23 +21,13 @@ NCH = T // CH
 FLOPS = 2 * M * K * N
 COUNT = K * N
 NWARM = 3
-NWARM2 = 0
 SUMW = 256
-LEAD = 3
-EARLY = 2
-
-
-def build_groups():
-    groups = [(t, 1, ((0, 0),) if t % 2 == 1 else ()) for t in range(4)]
-    for t in range(4, T, 2):
-        s_set = ((0, 0), (1, 0)) if t % 4 == 0 else ((0, 0),)
-        if t >= T - 4:
-            s_set = ((0, 0),) if t == T - 4 else ()
-        groups.append((t, 2, s_set))
-    return groups
-
-
-GROUPS = build_groups()
+GROUPS = (
+    [(0, 1, ((0, 0),)), (1, 1, ((0, 0),)), (2, 2, ((0, 0),))]
+    + [(t, 2, ((0, 0), (1, 0)) if t % 4 == 0 else ((0, 0),)) for t in range(4, 28, 2)]
+    + [(28, 2, ((0, 0),)), (30, 2, ())]
+)
+LEAD = 2
 
 
 def tile_ternarydense_t_kernel(tc, x, w, b, out):
@@ -45,9 +35,10 @@ def tile_ternarydense_t_kernel(tc, x, w, b, out):
     with ExitStack() as ctx:
         const = ctx.enter_context(tc.tile_pool(name="const", bufs=1))
         xin = ctx.enter_context(tc.tile_pool(name="xin", bufs=NCH))
-        grp = ctx.enter_context(tc.tile_pool(name="grp", bufs=NCH))
-        stage = ctx.enter_context(tc.tile_pool(name="stage", bufs=9))
-        ps_o = ctx.enter_context(tc.psum_pool(name="ps_o", bufs=8))
+        grp = ctx.enter_context(tc.tile_pool(name="grp", bufs=3))
+        stage = ctx.enter_context(tc.tile_pool(name="stage", bufs=12))
+        ps_t = ctx.enter_context(tc.psum_pool(name="ps_t", bufs=2))
+        ps_o = ctx.enter_context(tc.psum_pool(name="ps_o", bufs=6))
         ctx.enter_context(tc.manual_schedule())
 
         xv = x.rearrange("(p t) k -> p t k", t=T)
@@ -114,21 +105,21 @@ def tile_ternarydense_t_kernel(tc, x, w, b, out):
         x_scales = const.tile([P, T * P], U8, name="x_scales", align_bytes=64)
         groups = {}
 
-        def turn_x(i):
-            c, j = i // 2, i % 2
+        def turn_x(c):
             xw = x_raw[c][:].bitcast(F32)
-            if j == 0:
-                groups[c] = grp.tile([P, CH * K], BF16, name="g", align_bytes=64)
-            gw = groups[c][:].bitcast(F32)
-            xt = ps_o.tile([P, 2, 2, P], F32, name="xt", tag="acc")
-            for r in range(2):
-                for u in range(2):
-                    col = (2 * j + r) * 256 + u * P
-                    nc.tensor.transpose(xt[:, r, u, :], xw[:, col : col + P], ident[:])
-            nc.scalar.copy(
-                out=gw[:, j * 512 : (j + 1) * 512].rearrange("p (r m u) -> p r m u", r=2, u=2),
-                in_=xt[:].rearrange("p r u m -> p r m u"),
-            )
+            g = grp.tile([P, CH * K], BF16, name="g", align_bytes=64)
+            gw = g[:].bitcast(F32)
+            for j in range(CH // 2):
+                xt = ps_t.tile([P, 2, 2, P], F32, name="xt")
+                for r in range(2):
+                    for u in range(2):
+                        col = (2 * j + r) * 256 + u * P
+                        nc.tensor.transpose(xt[:, r, u, :], xw[:, col : col + P], ident[:])
+                nc.scalar.copy(
+                    out=gw[:, j * 512 : (j + 1) * 512].rearrange("p (r m u) -> p r m u", r=2, u=2),
+                    in_=xt[:].rearrange("p r u m -> p r m u"),
+                )
+            groups[c] = g
 
         def quantise_x(c):
             cs = slice(c * CH * P, (c + 1) * CH * P)
@@ -140,13 +131,11 @@ def tile_ternarydense_t_kernel(tc, x, w, b, out):
             pb = ps_o.tile([P, HALF], F32, name="pb", tag="acc")
             nc.tensor.matmul(pb[:], lhsT=ones[:], rhs=brow[:, h * HALF : (h + 1) * HALF], start=True, stop=True)
             pbs.append(pb)
-        for i in range(4):
-            turn_x(i)
+        turn_x(0)
         for h in range(2):
             nc.scalar.copy(out=b_bc[:, h * HALF : (h + 1) * HALF], in_=pbs[h][:])
-
-        for i in range(NWARM2):
-            nc.tensor.matmul(warm[:], lhsT=ones[:], rhs=zeros[:], start=True, stop=True)
+        turn_x(1)
+        turn_x(2)
 
         tot = const.tile([P, 1], F32, name="tot")
         nc.vector.tensor_reduce(out=tot[:], in_=psum_s[:], axis=AX.X, op=ALU.add)
@@ -157,32 +146,26 @@ def tile_ternarydense_t_kernel(tc, x, w, b, out):
         wt = const.tile([P, 4 * N], BF16, name="wt", align_bytes=64)
         w_codes = const.tile([P, N], U32, name="w_codes", align_bytes=64)
         w_scales = const.tile([P, N], U8, name="w_scales", align_bytes=64)
-        def w_step(h, i):
+        for h in range(2):
             sl = slice(h * 4 * HALF, (h + 1) * 4 * HALF)
             hs = slice(h * HALF, (h + 1) * HALF)
-            if i == 0:
-                nc.vector.tensor_scalar(
-                    out=t1[:, sl], in0=wg[:, sl], scalar1=sc[:, 0:1], scalar2=sc[:, 1:2], op0=ALU.is_ge, op1=ALU.mult
-                )
-            elif i == 1:
-                nc.vector.tensor_scalar(
-                    out=t2[:, sl], in0=wg[:, sl], scalar1=sc[:, 2:3], scalar2=sc[:, 3:4], op0=ALU.is_le, op1=ALU.mult
-                )
-            elif i == 2:
-                nc.vector.tensor_tensor(out=wt[:, sl], in0=t1[:, sl], in1=t2[:, sl], op=ALU.add)
-            else:
-                nc.vector.quantize_mx(out=w_codes[:, hs].bitcast(FP8X4), scales=w_scales[:, hs], in_=wt[:, sl])
-
-        for i in range(3):
-            w_step(0, i)
-        quantise_x(0)
-        w_step(0, 3)
+            nc.vector.tensor_scalar(
+                out=t1[:, sl], in0=wg[:, sl], scalar1=sc[:, 0:1], scalar2=sc[:, 1:2], op0=ALU.is_ge, op1=ALU.mult
+            )
+            nc.vector.tensor_scalar(
+                out=t2[:, sl], in0=wg[:, sl], scalar1=sc[:, 2:3], scalar2=sc[:, 3:4], op0=ALU.is_le, op1=ALU.mult
+            )
+            nc.vector.tensor_tensor(out=wt[:, sl], in0=t1[:, sl], in1=t2[:, sl], op=ALU.add)
+            quantise_x(h)
+            nc.vector.quantize_mx(out=w_codes[:, hs].bitcast(FP8X4), scales=w_scales[:, hs], in_=wt[:, sl])
 
         o_tiles = {}
 
-        accs = {}
-
-        def multiply(j, t, h):
+        def bank(j, t, h, who):
+            t0, nt = GROUPS[j][0], GROUPS[j][1]
+            if j not in o_tiles:
+                o_tiles[j] = stage.tile([P, nt, N], F32, name="o")
+            o = o_tiles[j]
             ts = slice(t * P, (t + 1) * P)
             hs = slice(h * HALF, (h + 1) * HALF)
             acc = ps_o.tile([P, HALF], F32, name="acc")
@@ -195,54 +178,29 @@ def tile_ternarydense_t_kernel(tc, x, w, b, out):
                 start=True,
                 stop=True,
             )
-            accs[(t, h)] = acc
-
-        def leave(j, t, h, who):
-            t0, nt = GROUPS[j][0], GROUPS[j][1]
-            if j not in o_tiles:
-                o_tiles[j] = stage.tile([P, nt, N], F32, name="o")
-            hs = slice(h * HALF, (h + 1) * HALF)
-            dst = o_tiles[j][:, t - t0, hs]
-            acc = accs[(t, h)]
             if who == "s":
-                nc.scalar.copy(out=dst, in_=acc[:])
-                nc.gpsimd.tensor_tensor(out=dst, in0=dst, in1=b_bc[:, hs], op=ALU.add)
+                nc.scalar.copy(out=o[:, t - t0, hs], in_=acc[:])
+                nc.gpsimd.tensor_tensor(out=o[:, t - t0, hs], in0=o[:, t - t0, hs], in1=b_bc[:, hs], op=ALU.add)
             else:
-                nc.vector.tensor_tensor(out=dst, in0=acc[:], in1=b_bc[:, hs], op=ALU.add)
+                nc.vector.tensor_tensor(out=o[:, t - t0, hs], in0=acc[:], in1=b_bc[:, hs], op=ALU.add)
 
         def banks_of(j, who):
             t0, nt, s_set = GROUPS[j]
-            return [(t, h) for t in range(t0, t0 + nt) for h in range(2) if ((t - t0, h) in s_set) == (who == "s")]
+            for t in range(t0, t0 + nt):
+                for h in range(2):
+                    if ((t - t0, h) in s_set) == (who == "s"):
+                        bank(j, t, h, who)
 
-        def s_banks(j):
-            for t, h in banks_of(j, "s"):
-                multiply(j, t, h)
-                leave(j, t, h, "s")
-
-        for j in range(4):
-            s_banks(j)
-            if j < EARLY:
-                turn_x(j + 4)
-        multiply(0, 0, 0)
-        for i in range(4):
-            w_step(1, i)
-        multiply(0, 0, 1)
-        s_done = 4
+        for j in range(LEAD):
+            banks_of(j, "s")
         for j in range(len(GROUPS)):
             t0, nt, s_set = GROUPS[j]
             c = t0 // CH
-            for t, h in banks_of(j, "v"):
-                leave(j, t, h, "v")
-            if t0 == 1:
-                quantise_x(1)
-            if (t0 == 3 or (t0 >= CH and t0 % CH == 0)) and c + 2 < NCH:
+            if t0 % CH == 0 and c + 2 < NCH:
                 quantise_x(c + 2)
-            if j + 1 < len(GROUPS):
-                for t, h in banks_of(j + 1, "v"):
-                    multiply(j + 1, t, h)
-            while s_done < len(GROUPS) and s_done <= max(j + LEAD, 5) and j >= (1 if s_done < 6 else 3):
-                s_banks(s_done)
-                s_done += 1
-            if j + 4 + EARLY < 2 * NCH:
-                turn_x(j + 4 + EARLY)
+            if j + LEAD < len(GROUPS):
+                banks_of(j + LEAD, "s")
+            if t0 % CH == 2 and c + 3 < NCH:
+                turn_x(c + 3)
+            banks_of(j, "v")
             nc.sync.dma_start(out=ov[:, t0 : t0 + nt, :], in_=o_tiles[j][:])

@@ -11,6 +11,7 @@ U8 = mybir.dt.uint8
 FP8X4 = mybir.dt.float8_e4m3fn_x4
 ALU = mybir.AluOpType
 AX = mybir.AxisListType
+ACT = mybir.ActivationFunctionType
 
 M, K, N = 4096, 512, 1024
 P = 128
@@ -20,13 +21,15 @@ CH = 4
 NCH = T // CH
 FLOPS = 2 * M * K * N
 COUNT = K * N
-NWARM = 3
-SUMW = 256
+NWARM = 4
+SUMW = 128
 GROUPS = (
-    [(0, 1, ((0, 0),)), (1, 1, ((0, 0),)), (2, 2, ((0, 0),))]
-    + [(t, 2, ((0, 0), (1, 0)) if t % 4 == 0 else ((0, 0),)) for t in range(4, 28, 2)]
+    [(0, 1, ()), (1, 1, ((0, 0),)), (2, 1, ()), (3, 1, ((0, 0),)), (4, 2, ((0, 0),)), (6, 2, ((0, 0),))]
+    + [(t, 2, ((0, 0), (1, 0)) if t % 4 == 0 else ((0, 0),)) for t in range(8, 28, 2)]
     + [(28, 2, ((0, 0),)), (30, 2, ())]
 )
+NV = 384
+AHEAD = 2
 LEAD = 2
 
 
@@ -49,9 +52,13 @@ def tile_ternarydense_t_kernel(tc, x, w, b, out):
         zeros = const.tile([P, HALF], BF16, name="zeros")
         nc.vector.memset(zeros[:].bitcast(I32), 0)
         brow = const.tile([P, N], BF16, name="brow")
-        nc.gpsimd.memset(brow[:], 0.0)
+        nc.gpsimd.memset(brow[:].bitcast(I32), 0)
         ident = const.tile([P, P], F32, name="ident")
         make_identity(nc, ident[:])
+        identb = const.tile([P, P], BF16, name="identb")
+        make_identity(nc, identb[:])
+        onesf = const.tile([P, P], F32, name="onesf")
+        nc.gpsimd.memset(onesf[:], 1.0)
         cst = const.tile([P, 4], F32, name="cst")
         nc.gpsimd.memset(cst[:, 0:1], 0.7 / COUNT)
         nc.gpsimd.memset(cst[:, 1:2], 1.0 / COUNT)
@@ -60,10 +67,11 @@ def tile_ternarydense_t_kernel(tc, x, w, b, out):
 
         w_raw = const.tile([P, 4 * N], BF16, name="w_raw")
         for u in range(2):
-            nc.sync.dma_start(
-                out=w_raw[:, u * 2 * N : (u + 1) * 2 * N].rearrange("p (e n) -> p e n", e=2),
-                in_=w[u * 256 : (u + 1) * 256, :].rearrange("(q e) n -> q e n", e=2),
-            )
+            for e in range(2):
+                nc.sync.dma_start(
+                    out=w_raw[:, (2 * u + e) * N : (2 * u + e + 1) * N],
+                    in_=w[u * 256 : (u + 1) * 256, :].rearrange("(q e) n -> q e n", e=2)[:, e, :],
+                )
         nc.sync.dma_start(out=brow[0:1, :], in_=b.unsqueeze(0))
         x_raw = []
         for c in range(NCH):
@@ -74,47 +82,60 @@ def tile_ternarydense_t_kernel(tc, x, w, b, out):
             )
             x_raw.append(xr)
 
+        tiny = const.tile([P, 1], BF16, name="tiny")
+        nc.scalar.copy(out=tiny[:], in_=ones[:, 0:1])
+
         warm = ps_o.tile([P, HALF], F32, name="warm", tag="acc")
         for i in range(NWARM):
             nc.tensor.matmul(warm[:], lhsT=ones[:], rhs=zeros[:], start=True, stop=True)
 
         aw = const.tile([P, 4 * N], BF16, name="aw")
-        psum_s = ps_o.tile([P, SUMW], F32, name="psum_s", tag="acc")
-        nsum = 4 * N // SUMW
-        for q in range(4):
+        asum = const.tile([P, 1], F32, name="asum")
+        nc.scalar.activation(out=aw[:, 0:N], in_=w_raw[:, 0:N], func=ACT.Abs, accum_out=asum[:])
+        psum_s = ps_o.tile([P, SUMW + 1], F32, name="psum_s", tag="acc")
+        nsum = 3 * N // SUMW
+        for q in range(1, 4):
             sl = slice(q * N, (q + 1) * N)
             nc.vector.tensor_single_scalar(
                 out=aw[:, sl].bitcast(I32), in_=w_raw[:, sl].bitcast(I32), scalar=0x7FFF7FFF, op=ALU.bitwise_and
             )
-            for c in range(q * nsum // 4, (q + 1) * nsum // 4):
+            for c in range((q - 1) * nsum // 3, q * nsum // 3):
                 nc.tensor.matmul(
-                    psum_s[:], lhsT=ones[:], rhs=aw[:, c * SUMW : (c + 1) * SUMW], start=(c == 0), stop=(c == nsum - 1)
+                    psum_s[:, 0:SUMW],
+                    lhsT=ones[:],
+                    rhs=aw[:, N + c * SUMW : N + (c + 1) * SUMW],
+                    start=(c == 0),
+                    stop=(c == nsum - 1),
                 )
+        nc.tensor.matmul(psum_s[:, SUMW : SUMW + 1], lhsT=onesf[:], rhs=asum[:], start=True, stop=True)
 
-        wg = const.tile([P, 4 * N], BF16, name="wg", align_bytes=64)
+        wg = const.tile([P, 4 * NV], BF16, name="wg", align_bytes=64)
         w_tn = w_raw[:].rearrange("p (t n) -> p t n", t=4)
-        for h in range(2):
-            dst = wg[:, h * 4 * HALF : (h + 1) * 4 * HALF].rearrange("p (c i t) -> p c t i", i=4, t=4)
-            src = w_tn[:, :, h * HALF : (h + 1) * HALF].rearrange("p t (c i) -> p c t i", i=4)
-            if h == 0:
-                nc.vector.tensor_copy(out=dst, in_=src)
-            else:
-                nc.scalar.copy(out=dst, in_=src)
+        nc.vector.tensor_copy(
+            out=wg[:].rearrange("p (c i t) -> p c t i", i=4, t=4),
+            in_=w_tn[:, :, 0:NV].rearrange("p t (c i) -> p c t i", i=4),
+        )
 
         x_codes = const.tile([P, T * P], U32, name="x_codes", align_bytes=64)
         x_scales = const.tile([P, T * P], U8, name="x_scales", align_bytes=64)
         groups = {}
+        turned = {}
 
         def turn_x(c):
             xw = x_raw[c][:].bitcast(F32)
-            g = grp.tile([P, CH * K], BF16, name="g", align_bytes=64)
-            gw = g[:].bitcast(F32)
+            turned[c] = []
             for j in range(CH // 2):
                 xt = ps_t.tile([P, 2, 2, P], F32, name="xt")
                 for r in range(2):
                     for u in range(2):
                         col = (2 * j + r) * 256 + u * P
                         nc.tensor.transpose(xt[:, r, u, :], xw[:, col : col + P], ident[:])
+                turned[c].append(xt)
+
+        def copy_x(c):
+            g = grp.tile([P, CH * K], BF16, name="g", align_bytes=64)
+            gw = g[:].bitcast(F32)
+            for j, xt in enumerate(turned[c]):
                 nc.scalar.copy(
                     out=gw[:, j * 512 : (j + 1) * 512].rearrange("p (r m u) -> p r m u", r=2, u=2),
                     in_=xt[:].rearrange("p r u m -> p r m u"),
@@ -132,40 +153,64 @@ def tile_ternarydense_t_kernel(tc, x, w, b, out):
             nc.tensor.matmul(pb[:], lhsT=ones[:], rhs=brow[:, h * HALF : (h + 1) * HALF], start=True, stop=True)
             pbs.append(pb)
         turn_x(0)
-        for h in range(2):
-            nc.scalar.copy(out=b_bc[:, h * HALF : (h + 1) * HALF], in_=pbs[h][:])
-        turn_x(1)
-        turn_x(2)
+        copy_x(0)
 
         tot = const.tile([P, 1], F32, name="tot")
         nc.vector.tensor_reduce(out=tot[:], in_=psum_s[:], axis=AX.X, op=ALU.add)
         sc = const.tile([P, 4], F32, name="sc")
         nc.vector.tensor_scalar(out=sc[:], in0=cst[:], scalar1=tot[:, 0:1], scalar2=None, op0=ALU.mult)
-        t1 = const.tile([P, 4 * N], BF16, name="t1")
-        t2 = const.tile([P, 4 * N], BF16, name="t2")
+        t1r = const.tile([P, 4, N - NV], BF16, name="t1r")
+        t2r = const.tile([P, 4, N - NV], BF16, name="t2r")
+        t1 = const.tile([P, 4 * NV], BF16, name="t1")
+        t2 = const.tile([P, 4 * NV], BF16, name="t2")
         wt = const.tile([P, 4 * N], BF16, name="wt", align_bytes=64)
         w_codes = const.tile([P, N], U32, name="w_codes", align_bytes=64)
         w_scales = const.tile([P, N], U8, name="w_scales", align_bytes=64)
-        for h in range(2):
+
+        def above(dst, src):
+            nc.vector.tensor_scalar(
+                out=dst, in0=src, scalar1=sc[:, 0:1], scalar2=sc[:, 1:2], op0=ALU.is_ge, op1=ALU.mult
+            )
+
+        def below(dst, src):
+            nc.vector.tensor_scalar(
+                out=dst, in0=src, scalar1=sc[:, 2:3], scalar2=sc[:, 3:4], op0=ALU.is_le, op1=ALU.mult
+            )
+
+        def quantise_w(h):
             sl = slice(h * 4 * HALF, (h + 1) * 4 * HALF)
             hs = slice(h * HALF, (h + 1) * HALF)
-            nc.vector.tensor_scalar(
-                out=t1[:, sl], in0=wg[:, sl], scalar1=sc[:, 0:1], scalar2=sc[:, 1:2], op0=ALU.is_ge, op1=ALU.mult
-            )
-            nc.vector.tensor_scalar(
-                out=t2[:, sl], in0=wg[:, sl], scalar1=sc[:, 2:3], scalar2=sc[:, 3:4], op0=ALU.is_le, op1=ALU.mult
-            )
-            nc.vector.tensor_tensor(out=wt[:, sl], in0=t1[:, sl], in1=t2[:, sl], op=ALU.add)
-            quantise_x(h)
             nc.vector.quantize_mx(out=w_codes[:, hs].bitcast(FP8X4), scales=w_scales[:, hs], in_=wt[:, sl])
 
-        o_tiles = {}
+        for lo, hi in ((0, 2 * P), (2 * P, N - NV)):
+            above(t1r[:, :, lo:hi], w_tn[:, :, NV + lo : NV + hi])
+            below(t2r[:, :, lo:hi], w_tn[:, :, NV + lo : NV + hi])
+        for c in range((N - NV) // P):
+            wp = ps_o.tile([P, 4, P], F32, name="wp", tag="acc")
+            for t in range(4):
+                for i, part in enumerate((t1r, t2r)):
+                    nc.tensor.matmul(
+                        wp[:, t, :], lhsT=identb[:], rhs=part[:, t, c * P : (c + 1) * P], start=(i == 0), stop=(i == 1)
+                    )
+            if c == 0:
+                nc.scalar.copy(out=b_bc[:, 0:HALF], in_=pbs[0][:])
+            nc.scalar.copy(
+                out=wt[:, 4 * (NV + c * P) : 4 * (NV + (c + 1) * P)].rearrange("p (n t) -> p n t", t=4),
+                in_=wp[:].rearrange("p t n -> p n t"),
+            )
+        nc.scalar.copy(out=b_bc[:, HALF:N], in_=pbs[1][:])
+        above(t1[:], wg[:])
+        below(t2[:], wg[:])
+        quantise_x(0)
+        nc.vector.tensor_tensor(out=wt[:, 0 : 4 * NV], in0=t1[:], in1=t2[:], op=ALU.add)
+        quantise_w(0)
+        quantise_w(1)
+        turn_x(1)
 
-        def bank(j, t, h, who):
-            t0, nt = GROUPS[j][0], GROUPS[j][1]
-            if j not in o_tiles:
-                o_tiles[j] = stage.tile([P, nt, N], F32, name="o")
-            o = o_tiles[j]
+        o_tiles = {}
+        accs = {}
+
+        def multiply(t, h):
             ts = slice(t * P, (t + 1) * P)
             hs = slice(h * HALF, (h + 1) * HALF)
             acc = ps_o.tile([P, HALF], F32, name="acc")
@@ -178,29 +223,50 @@ def tile_ternarydense_t_kernel(tc, x, w, b, out):
                 start=True,
                 stop=True,
             )
-            if who == "s":
-                nc.scalar.copy(out=o[:, t - t0, hs], in_=acc[:])
-                nc.gpsimd.tensor_tensor(out=o[:, t - t0, hs], in0=o[:, t - t0, hs], in1=b_bc[:, hs], op=ALU.add)
-            else:
-                nc.vector.tensor_tensor(out=o[:, t - t0, hs], in0=acc[:], in1=b_bc[:, hs], op=ALU.add)
+            accs[t, h] = acc
 
-        def banks_of(j, who):
+        def target(j, t, h):
+            if j not in o_tiles:
+                o_tiles[j] = stage.tile([P, GROUPS[j][1], N], F32, name="o")
+            return o_tiles[j][:, t - GROUPS[j][0], h * HALF : (h + 1) * HALF]
+
+        def banks_of(j, scalar):
             t0, nt, s_set = GROUPS[j]
-            for t in range(t0, t0 + nt):
-                for h in range(2):
-                    if ((t - t0, h) in s_set) == (who == "s"):
-                        bank(j, t, h, who)
+            return [(j, t, h) for t in range(t0, t0 + nt) for h in range(2) if ((t - t0, h) in s_set) == scalar]
 
-        for j in range(LEAD):
-            banks_of(j, "s")
+        def scalar_banks(j):
+            for jj, t, h in banks_of(j, True):
+                multiply(t, h)
+                o = target(j, t, h)
+                nc.scalar.copy(out=o, in_=accs[t, h][:])
+                nc.gpsimd.tensor_tensor(out=o, in0=o, in1=b_bc[:, h * HALF : (h + 1) * HALF], op=ALU.add)
+
+        v_list = [bank for j in range(len(GROUPS)) for bank in banks_of(j, False)]
+
+        def vector_bank(i):
+            if i + AHEAD < len(v_list):
+                multiply(*v_list[i + AHEAD][1:])
+            j, t, h = v_list[i]
+            nc.vector.tensor_tensor(
+                out=target(j, t, h), in0=accs[t, h][:], in1=b_bc[:, h * HALF : (h + 1) * HALF], op=ALU.add
+            )
+
+        multiply(0, 0)
+        copy_x(1)
+        scalar_banks(1)
+        for i in range(1, AHEAD):
+            multiply(*v_list[i][1:])
+        i = 0
         for j in range(len(GROUPS)):
             t0, nt, s_set = GROUPS[j]
-            c = t0 // CH
-            if t0 % CH == 0 and c + 2 < NCH:
-                quantise_x(c + 2)
-            if j + LEAD < len(GROUPS):
-                banks_of(j + LEAD, "s")
-            if t0 % CH == 2 and c + 3 < NCH:
-                turn_x(c + 3)
-            banks_of(j, "v")
+            if j > 0 and j % 2 == 0 and j // 2 < NCH:
+                quantise_x(j // 2)
+            for k in range(len(banks_of(j, False))):
+                vector_bank(i)
+                i += 1
             nc.sync.dma_start(out=ov[:, t0 : t0 + nt, :], in_=o_tiles[j][:])
+            if 0 < j < len(GROUPS) - LEAD:
+                scalar_banks(j + LEAD)
+            if j % 2 == 1 and (j + 3) // 2 < NCH:
+                turn_x((j + 3) // 2)
+                copy_x((j + 3) // 2)

@@ -23,11 +23,14 @@ FLOPS = 2 * M * K * N
 COUNT = K * N
 NWARM = 4
 SUMW = 128
+RAMP = 8
 GROUPS = (
-    [(0, 1, ()), (1, 1, ((0, 0),)), (2, 1, ()), (3, 1, ((0, 0),)), (4, 2, ((0, 0),)), (6, 2, ((0, 0),))]
-    + [(t, 2, ((0, 0), (1, 0)) if t % 4 == 0 else ((0, 0),)) for t in range(8, 28, 2)]
+    [(t, 1, ((0, 0),) if t % 2 == 1 else ()) for t in range(RAMP)]
+    + [(t, 2, ((0, 0), (1, 0)) if t % 4 == 0 else ((0, 0),)) for t in range(RAMP, 28, 2)]
     + [(28, 2, ((0, 0),)), (30, 2, ())]
 )
+QUANTISE_AT = {2: 1, 6: 2, 8: 3, 10: 4, 12: 5, 14: 6, 16: 7}
+TURN_AT = {1: 2, 5: 3, 7: 4, 9: 5, 11: 6, 13: 7}
 NV = 384
 AHEAD = 2
 LEAD = 2
@@ -57,13 +60,15 @@ def tile_ternarydense_t_kernel(tc, x, w, b, out):
         make_identity(nc, ident[:])
         identb = const.tile([P, P], BF16, name="identb")
         make_identity(nc, identb[:])
-        onesf = const.tile([P, P], F32, name="onesf")
-        nc.gpsimd.memset(onesf[:], 1.0)
+        mean = const.tile([P, P], BF16, name="mean")
+        nc.gpsimd.memset(mean[:], 1.0 / COUNT)
+        meanf = const.tile([P, P], F32, name="meanf")
+        nc.gpsimd.memset(meanf[:], 1.0 / COUNT)
         cst = const.tile([P, 4], F32, name="cst")
-        nc.gpsimd.memset(cst[:, 0:1], 0.7 / COUNT)
-        nc.gpsimd.memset(cst[:, 1:2], 1.0 / COUNT)
-        nc.gpsimd.memset(cst[:, 2:3], -0.7 / COUNT)
-        nc.gpsimd.memset(cst[:, 3:4], -1.0 / COUNT)
+        nc.gpsimd.memset(cst[:, 0:1], 0.7)
+        nc.gpsimd.memset(cst[:, 1:2], 1.0)
+        nc.gpsimd.memset(cst[:, 2:3], -0.7)
+        nc.gpsimd.memset(cst[:, 3:4], -1.0)
 
         w_raw = const.tile([P, 4 * N], BF16, name="w_raw")
         for u in range(2):
@@ -72,7 +77,8 @@ def tile_ternarydense_t_kernel(tc, x, w, b, out):
                     out=w_raw[:, (2 * u + e) * N : (2 * u + e + 1) * N],
                     in_=w[u * 256 : (u + 1) * 256, :].rearrange("(q e) n -> q e n", e=2)[:, e, :],
                 )
-        nc.sync.dma_start(out=brow[0:1, :], in_=b.unsqueeze(0))
+            if u == 0:
+                nc.sync.dma_start(out=brow[0:1, :], in_=b.unsqueeze(0))
         x_raw = []
         for c in range(NCH):
             xr = xin.tile([P, CH * K], BF16, name="xr")
@@ -89,25 +95,36 @@ def tile_ternarydense_t_kernel(tc, x, w, b, out):
         for i in range(NWARM):
             nc.tensor.matmul(warm[:], lhsT=ones[:], rhs=zeros[:], start=True, stop=True)
 
+        b_bc = const.tile([P, N], F32, name="b_bc")
+        pbs = []
+        for h in range(2):
+            pb = ps_o.tile([P, HALF], F32, name="pb", tag="acc")
+            nc.tensor.matmul(pb[:], lhsT=ones[:], rhs=brow[:, h * HALF : (h + 1) * HALF], start=True, stop=True)
+            pbs.append(pb)
+
         aw = const.tile([P, 4 * N], BF16, name="aw")
-        asum = const.tile([P, 1], F32, name="asum")
-        nc.scalar.activation(out=aw[:, 0:N], in_=w_raw[:, 0:N], func=ACT.Abs, accum_out=asum[:])
-        psum_s = ps_o.tile([P, SUMW + 1], F32, name="psum_s", tag="acc")
-        nsum = 3 * N // SUMW
-        for q in range(1, 4):
+        asum = const.tile([P, 2], F32, name="asum")
+        for q in range(2):
+            sl = slice(q * N, (q + 1) * N)
+            nc.scalar.activation(out=aw[:, sl], in_=w_raw[:, sl], func=ACT.Abs, accum_out=asum[:, q : q + 1])
+        psum_s = ps_o.tile([P, SUMW + 2], F32, name="psum_s", tag="acc")
+        nsum = 2 * N // SUMW
+        for q in range(2, 4):
             sl = slice(q * N, (q + 1) * N)
             nc.vector.tensor_single_scalar(
                 out=aw[:, sl].bitcast(I32), in_=w_raw[:, sl].bitcast(I32), scalar=0x7FFF7FFF, op=ALU.bitwise_and
             )
-            for c in range((q - 1) * nsum // 3, q * nsum // 3):
+            for c in range((q - 2) * nsum // 2, (q - 1) * nsum // 2):
                 nc.tensor.matmul(
                     psum_s[:, 0:SUMW],
-                    lhsT=ones[:],
-                    rhs=aw[:, N + c * SUMW : N + (c + 1) * SUMW],
+                    lhsT=mean[:],
+                    rhs=aw[:, 2 * N + c * SUMW : 2 * N + (c + 1) * SUMW],
                     start=(c == 0),
                     stop=(c == nsum - 1),
                 )
-        nc.tensor.matmul(psum_s[:, SUMW : SUMW + 1], lhsT=onesf[:], rhs=asum[:], start=True, stop=True)
+        nc.tensor.matmul(psum_s[:, SUMW : SUMW + 2], lhsT=meanf[:], rhs=asum[:], start=True, stop=True)
+        for h in range(2):
+            nc.scalar.copy(out=b_bc[:, h * HALF : (h + 1) * HALF], in_=pbs[h][:])
 
         wg = const.tile([P, 4 * NV], BF16, name="wg", align_bytes=64)
         w_tn = w_raw[:].rearrange("p (t n) -> p t n", t=4)
@@ -146,19 +163,14 @@ def tile_ternarydense_t_kernel(tc, x, w, b, out):
             cs = slice(c * CH * P, (c + 1) * CH * P)
             nc.vector.quantize_mx(out=x_codes[:, cs].bitcast(FP8X4), scales=x_scales[:, cs], in_=groups[c][:])
 
-        b_bc = const.tile([P, N], F32, name="b_bc")
-        pbs = []
-        for h in range(2):
-            pb = ps_o.tile([P, HALF], F32, name="pb", tag="acc")
-            nc.tensor.matmul(pb[:], lhsT=ones[:], rhs=brow[:, h * HALF : (h + 1) * HALF], start=True, stop=True)
-            pbs.append(pb)
         turn_x(0)
         copy_x(0)
 
-        tot = const.tile([P, 1], F32, name="tot")
-        nc.vector.tensor_reduce(out=tot[:], in_=psum_s[:], axis=AX.X, op=ALU.add)
+        alpha = const.tile([P, 1], F32, name="alpha")
+        nc.vector.tensor_reduce(out=alpha[:], in_=psum_s[:], axis=AX.X, op=ALU.add)
+        apos = const.tile([P, P], BF16, name="apos")
+        aneg = const.tile([P, P], BF16, name="aneg")
         sc = const.tile([P, 4], F32, name="sc")
-        nc.vector.tensor_scalar(out=sc[:], in0=cst[:], scalar1=tot[:, 0:1], scalar2=None, op0=ALU.mult)
         t1r = const.tile([P, 4, N - NV], BF16, name="t1r")
         t2r = const.tile([P, 4, N - NV], BF16, name="t2r")
         t1 = const.tile([P, 4 * NV], BF16, name="t1")
@@ -182,27 +194,43 @@ def tile_ternarydense_t_kernel(tc, x, w, b, out):
             hs = slice(h * HALF, (h + 1) * HALF)
             nc.vector.quantize_mx(out=w_codes[:, hs].bitcast(FP8X4), scales=w_scales[:, hs], in_=wt[:, sl])
 
-        for lo, hi in ((0, 2 * P), (2 * P, N - NV)):
-            above(t1r[:, :, lo:hi], w_tn[:, :, NV + lo : NV + hi])
-            below(t2r[:, :, lo:hi], w_tn[:, :, NV + lo : NV + hi])
+        def is_above(dst, src, sign):
+            nc.vector.tensor_scalar(
+                out=dst, in0=src, scalar1=sign / 0.7, scalar2=alpha[:, 0:1], op0=ALU.mult, op1=ALU.is_ge
+            )
+
+        def raw_above(lo, hi):
+            is_above(t1r[:, :, lo * P : hi * P], w_tn[:, :, NV + lo * P : NV + hi * P], 1.0)
+
+        def raw_below(lo, hi):
+            is_above(t2r[:, :, lo * P : hi * P], w_tn[:, :, NV + lo * P : NV + hi * P], -1.0)
+
+        raw_above(0, 1)
+        nc.vector.tensor_scalar(out=apos[:], in0=identb[:], scalar1=alpha[:, 0:1], scalar2=None, op0=ALU.mult)
+        raw_below(0, 1)
+        nc.vector.tensor_scalar(
+            out=aneg[:], in0=identb[:], scalar1=alpha[:, 0:1], scalar2=-1.0, op0=ALU.mult, op1=ALU.mult
+        )
+        nc.vector.tensor_scalar(out=sc[:], in0=cst[:], scalar1=alpha[:, 0:1], scalar2=None, op0=ALU.mult)
+        raw_above(1, 3)
+        raw_below(1, 3)
+        above(t1[:], wg[:])
+        raw_above(3, 5)
+        below(t2[:], wg[:])
+        raw_below(3, 5)
+        nc.vector.tensor_tensor(out=wt[:, 0 : 4 * NV], in0=t1[:], in1=t2[:], op=ALU.add)
+        quantise_x(0)
         for c in range((N - NV) // P):
             wp = ps_o.tile([P, 4, P], F32, name="wp", tag="acc")
             for t in range(4):
-                for i, part in enumerate((t1r, t2r)):
+                for i, (factor, part) in enumerate(((apos, t1r), (aneg, t2r))):
                     nc.tensor.matmul(
-                        wp[:, t, :], lhsT=identb[:], rhs=part[:, t, c * P : (c + 1) * P], start=(i == 0), stop=(i == 1)
+                        wp[:, t, :], lhsT=factor[:], rhs=part[:, t, c * P : (c + 1) * P], start=(i == 0), stop=(i == 1)
                     )
-            if c == 0:
-                nc.scalar.copy(out=b_bc[:, 0:HALF], in_=pbs[0][:])
             nc.scalar.copy(
                 out=wt[:, 4 * (NV + c * P) : 4 * (NV + (c + 1) * P)].rearrange("p (n t) -> p n t", t=4),
                 in_=wp[:].rearrange("p t n -> p n t"),
             )
-        nc.scalar.copy(out=b_bc[:, HALF:N], in_=pbs[1][:])
-        above(t1[:], wg[:])
-        below(t2[:], wg[:])
-        quantise_x(0)
-        nc.vector.tensor_tensor(out=wt[:, 0 : 4 * NV], in0=t1[:], in1=t2[:], op=ALU.add)
         quantise_w(0)
         quantise_w(1)
         turn_x(1)
@@ -252,21 +280,25 @@ def tile_ternarydense_t_kernel(tc, x, w, b, out):
             )
 
         multiply(0, 0)
-        copy_x(1)
         scalar_banks(1)
+        copy_x(1)
         for i in range(1, AHEAD):
             multiply(*v_list[i][1:])
         i = 0
         for j in range(len(GROUPS)):
             t0, nt, s_set = GROUPS[j]
-            if j > 0 and j % 2 == 0 and j // 2 < NCH:
-                quantise_x(j // 2)
+            if j in QUANTISE_AT:
+                quantise_x(QUANTISE_AT[j])
             for k in range(len(banks_of(j, False))):
                 vector_bank(i)
                 i += 1
-            nc.sync.dma_start(out=ov[:, t0 : t0 + nt, :], in_=o_tiles[j][:])
+                if j == 0:
+                    ks = slice(k * HALF, (k + 1) * HALF)
+                    nc.sync.dma_start(out=ov[:, t0, ks], in_=o_tiles[j][:, 0, ks])
+            if j > 0:
+                nc.sync.dma_start(out=ov[:, t0 : t0 + nt, :], in_=o_tiles[j][:])
             if 0 < j < len(GROUPS) - LEAD:
                 scalar_banks(j + LEAD)
-            if j % 2 == 1 and (j + 3) // 2 < NCH:
-                turn_x((j + 3) // 2)
-                copy_x((j + 3) // 2)
+            if j in TURN_AT:
+                turn_x(TURN_AT[j])
+                copy_x(TURN_AT[j])

@@ -50,25 +50,25 @@ def tile_ternarydense_t_kernel(tc, x, w, b, out):
         xv = x.rearrange("(p t) k -> p t k", t=T)
         ov = out.rearrange("(p t) n -> p t n", t=T)
 
+        ident = const.tile([P, P], F32, name="ident")
+        make_identity(nc, ident[:])
         ones = const.tile([P, P], BF16, name="ones")
         nc.vector.memset(ones[:], 1.0)
         zeros = const.tile([P, HALF], BF16, name="zeros")
         nc.vector.memset(zeros[:].bitcast(I32), 0)
         brow = const.tile([P, N], BF16, name="brow")
-        nc.gpsimd.memset(brow[:].bitcast(I32), 0)
-        ident = const.tile([P, P], F32, name="ident")
-        make_identity(nc, ident[:])
-        identb = const.tile([P, P], BF16, name="identb")
-        make_identity(nc, identb[:])
+        nc.vector.memset(brow[:].bitcast(I32), 0)
         mean = const.tile([P, P], BF16, name="mean")
-        nc.gpsimd.memset(mean[:], 1.0 / COUNT)
+        nc.vector.memset(mean[:], 1.0 / COUNT)
         meanf = const.tile([P, P], F32, name="meanf")
-        nc.gpsimd.memset(meanf[:], 1.0 / COUNT)
+        nc.vector.memset(meanf[:], 1.0 / COUNT)
         cst = const.tile([P, 4], F32, name="cst")
-        nc.gpsimd.memset(cst[:, 0:1], 0.7)
-        nc.gpsimd.memset(cst[:, 1:2], 1.0)
-        nc.gpsimd.memset(cst[:, 2:3], -0.7)
-        nc.gpsimd.memset(cst[:, 3:4], -1.0)
+        nc.vector.memset(cst[:, 0:1], 0.7)
+        nc.vector.memset(cst[:, 1:2], 1.0)
+        nc.vector.memset(cst[:, 2:3], -0.7)
+        nc.vector.memset(cst[:, 3:4], -1.0)
+        identb = const.tile([P, P], BF16, name="identb")
+        nc.vector.tensor_copy(out=identb[:], in_=ident[:])
 
         w_raw = const.tile([P, 4 * N], BF16, name="w_raw")
         for u in range(2):

@@ -21,16 +21,17 @@ CH = 4
 NCH = T // CH
 FLOPS = 2 * M * K * N
 COUNT = K * N
-NWARM = 4
+NWARM = 16
 SUMW = 128
 RAMP = 8
 GROUPS = (
     [(t, 1, ((0, 0),) if t % 2 == 1 else ()) for t in range(RAMP)]
-    + [(t, 2, ((0, 0), (1, 0)) if t % 4 == 0 else ((0, 0),)) for t in range(RAMP, 28, 2)]
+    + [(t, 2, ((0, 0), (1, 0)) if t % 4 == 0 and t > RAMP else ((0, 0),)) for t in range(RAMP, 28, 2)]
     + [(28, 2, ((0, 0),)), (30, 2, ())]
 )
-QUANTISE_AT = {2: 1, 6: 2, 8: 3, 10: 4, 12: 5, 14: 6, 16: 7}
-TURN_AT = {1: 2, 5: 3, 7: 4, 9: 5, 11: 6, 13: 7}
+QUANTISE_AT = {4: 2, 8: 3, 10: 4, 12: 5, 14: 6, 16: 7}
+TURN_AT = {0: 2, 5: 3, 7: 4, 9: 5, 11: 6, 13: 7}
+SCALAR_AFTER = {1: (3,), 4: (5,), 5: (7,)}
 NV = 384
 AHEAD = 2
 LEAD = 2
@@ -54,8 +55,6 @@ def tile_ternarydense_t_kernel(tc, x, w, b, out):
         make_identity(nc, ident[:])
         ones = const.tile([P, P], BF16, name="ones")
         nc.vector.memset(ones[:], 1.0)
-        zeros = const.tile([P, HALF], BF16, name="zeros")
-        nc.vector.memset(zeros[:].bitcast(I32), 0)
         brow = const.tile([P, N], BF16, name="brow")
         nc.vector.memset(brow[:].bitcast(I32), 0)
         mean = const.tile([P, P], BF16, name="mean")
@@ -91,9 +90,9 @@ def tile_ternarydense_t_kernel(tc, x, w, b, out):
         tiny = const.tile([P, 1], BF16, name="tiny")
         nc.scalar.copy(out=tiny[:], in_=ones[:, 0:1])
 
-        warm = ps_o.tile([P, HALF], F32, name="warm", tag="acc")
+        warm = ps_o.tile([P, P], F32, name="warm", tag="acc")
         for i in range(NWARM):
-            nc.tensor.matmul(warm[:], lhsT=ones[:], rhs=zeros[:], start=True, stop=True)
+            nc.tensor.matmul(warm[:], lhsT=ones[:], rhs=ones[:], start=True, stop=True)
 
         b_bc = const.tile([P, N], F32, name="b_bc")
         pbs = []
@@ -280,8 +279,8 @@ def tile_ternarydense_t_kernel(tc, x, w, b, out):
             )
 
         multiply(0, 0)
-        scalar_banks(1)
         copy_x(1)
+        scalar_banks(1)
         for i in range(1, AHEAD):
             multiply(*v_list[i][1:])
         i = 0
@@ -293,12 +292,14 @@ def tile_ternarydense_t_kernel(tc, x, w, b, out):
                 vector_bank(i)
                 i += 1
                 if j == 0:
+                    if k == 0:
+                        quantise_x(1)
                     ks = slice(k * HALF, (k + 1) * HALF)
                     nc.sync.dma_start(out=ov[:, t0, ks], in_=o_tiles[j][:, 0, ks])
             if j > 0:
                 nc.sync.dma_start(out=ov[:, t0 : t0 + nt, :], in_=o_tiles[j][:])
-            if 0 < j < len(GROUPS) - LEAD:
-                scalar_banks(j + LEAD)
+            for jj in SCALAR_AFTER.get(j, [j + LEAD] if RAMP - LEAD <= j < len(GROUPS) - LEAD else []):
+                scalar_banks(jj)
             if j in TURN_AT:
                 turn_x(TURN_AT[j])
                 copy_x(TURN_AT[j])

from contextlib import ExitStack

import concourse.mybir as mybir
from concourse.masks import make_identity

F32 = mybir.dt.float32
BF16 = mybir.dt.bfloat16
I32 = mybir.dt.int32
U32 = mybir.dt.uint32
U8 = mybir.dt.uint8
FP8X4 = mybir.dt.float8_e4m3fn_x4
ALU = mybir.AluOpType
AX = mybir.AxisListType
ACT = mybir.ActivationFunctionType

M, K, N = 4096, 512, 1024
P = 128
T = M // P
HALF = 512
CH = 4
NCH = T // CH
FLOPS = 2 * M * K * N
COUNT = K * N
NWARM = 16
SUMW = 128
RAMP = 8
GROUPS = (
    [(t, 1, ((0, 0),) if t % 2 == 1 else ()) for t in range(RAMP)]
    + [(t, 2, ((0, 0), (1, 0)) if t % 4 == 0 and t > RAMP else ((0, 0),)) for t in range(RAMP, 28, 2)]
    + [(28, 2, ((0, 0),)), (30, 2, ())]
)
QUANTISE_AT = {4: 2, 8: 3, 10: 4, 12: 5, 14: 6, 16: 7}
TURN_AT = {0: 2, 5: 3, 7: 4, 9: 5, 11: 6, 13: 7}
SCALAR_AFTER = {1: (3,), 4: (5,), 5: (7,)}
NV = 384
AHEAD = 2
LEAD = 2


def tile_ternarydense_t_kernel(tc, x, w, b, out):
    nc = tc.nc
    with ExitStack() as ctx:
        const = ctx.enter_context(tc.tile_pool(name="const", bufs=1))
        xin = ctx.enter_context(tc.tile_pool(name="xin", bufs=NCH))
        grp = ctx.enter_context(tc.tile_pool(name="grp", bufs=3))
        stage = ctx.enter_context(tc.tile_pool(name="stage", bufs=12))
        ps_t = ctx.enter_context(tc.psum_pool(name="ps_t", bufs=2))
        ps_o = ctx.enter_context(tc.psum_pool(name="ps_o", bufs=6))
        ctx.enter_context(tc.manual_schedule())

        xv = x.rearrange("(p t) k -> p t k", t=T)
        ov = out.rearrange("(p t) n -> p t n", t=T)

        ident = const.tile([P, P], F32, name="ident")
        make_identity(nc, ident[:])
        ones = const.tile([P, P], BF16, name="ones")
        nc.vector.memset(ones[:], 1.0)
        brow = const.tile([P, N], BF16, name="brow")
        nc.vector.memset(brow[:].bitcast(I32), 0)
        mean = const.tile([P, P], BF16, name="mean")
        nc.vector.memset(mean[:], 1.0 / COUNT)
        meanf = const.tile([P, P], F32, name="meanf")
        nc.vector.memset(meanf[:], 1.0 / COUNT)
        cst = const.tile([P, 4], F32, name="cst")
        nc.vector.memset(cst[:, 0:1], 0.7)
        nc.vector.memset(cst[:, 1:2], 1.0)
        nc.vector.memset(cst[:, 2:3], -0.7)
        nc.vector.memset(cst[:, 3:4], -1.0)
        identb = const.tile([P, P], BF16, name="identb")
        nc.vector.tensor_copy(out=identb[:], in_=ident[:])

        w_raw = const.tile([P, 4 * N], BF16, name="w_raw")
        for u in range(2):
            for e in range(2):
                nc.sync.dma_start(
                    out=w_raw[:, (2 * u + e) * N : (2 * u + e + 1) * N],
                    in_=w[u * 256 : (u + 1) * 256, :].rearrange("(q e) n -> q e n", e=2)[:, e, :],
                )
            if u == 0:
                nc.sync.dma_start(out=brow[0:1, :], in_=b.unsqueeze(0))
        x_raw = []
        for c in range(NCH):
            xr = xin.tile([P, CH * K], BF16, name="xr")
            nc.sync.dma_start(
                out=xr[:].rearrange("p (t k) -> p t k", t=CH),
                in_=xv[:, c * CH : (c + 1) * CH, :],
            )
            x_raw.append(xr)

        tiny = const.tile([P, 1], BF16, name="tiny")
        nc.scalar.copy(out=tiny[:], in_=ones[:, 0:1])

        warm = ps_o.tile([P, P], F32, name="warm", tag="acc")
        for i in range(NWARM):
            nc.tensor.matmul(warm[:], lhsT=ones[:], rhs=ones[:], start=True, stop=True)

        b_bc = const.tile([P, N], F32, name="b_bc")
        pbs = []
        for h in range(2):
            pb = ps_o.tile([P, HALF], F32, name="pb", tag="acc")
            nc.tensor.matmul(pb[:], lhsT=ones[:], rhs=brow[:, h * HALF : (h + 1) * HALF], start=True, stop=True)
            pbs.append(pb)

        aw = const.tile([P, 4 * N], BF16, name="aw")
        asum = const.tile([P, 2], F32, name="asum")
        for q in range(2):
            sl = slice(q * N, (q + 1) * N)
            nc.scalar.activation(out=aw[:, sl], in_=w_raw[:, sl], func=ACT.Abs, accum_out=asum[:, q : q + 1])
        psum_s = ps_o.tile([P, SUMW + 2], F32, name="psum_s", tag="acc")
        nsum = 2 * N // SUMW
        for q in range(2, 4):
            sl = slice(q * N, (q + 1) * N)
            nc.vector.tensor_single_scalar(
                out=aw[:, sl].bitcast(I32), in_=w_raw[:, sl].bitcast(I32), scalar=0x7FFF7FFF, op=ALU.bitwise_and
            )
            for c in range((q - 2) * nsum // 2, (q - 1) * nsum // 2):
                nc.tensor.matmul(
                    psum_s[:, 0:SUMW],
                    lhsT=mean[:],
                    rhs=aw[:, 2 * N + c * SUMW : 2 * N + (c + 1) * SUMW],
                    start=(c == 0),
                    stop=(c == nsum - 1),
                )
        nc.tensor.matmul(psum_s[:, SUMW : SUMW + 2], lhsT=meanf[:], rhs=asum[:], start=True, stop=True)
        for h in range(2):
            nc.scalar.copy(out=b_bc[:, h * HALF : (h + 1) * HALF], in_=pbs[h][:])

        wg = const.tile([P, 4 * NV], BF16, name="wg", align_bytes=64)
        w_tn = w_raw[:].rearrange("p (t n) -> p t n", t=4)
        nc.vector.tensor_copy(
            out=wg[:].rearrange("p (c i t) -> p c t i", i=4, t=4),
            in_=w_tn[:, :, 0:NV].rearrange("p t (c i) -> p c t i", i=4),
        )

        x_codes = const.tile([P, T * P], U32, name="x_codes", align_bytes=64)
        x_scales = const.tile([P, T * P], U8, name="x_scales", align_bytes=64)
        groups = {}
        turned = {}

        def turn_x(c):
            xw = x_raw[c][:].bitcast(F32)
            turned[c] = []
            for j in range(CH // 2):
                xt = ps_t.tile([P, 2, 2, P], F32, name="xt")
                for r in range(2):
                    for u in range(2):
                        col = (2 * j + r) * 256 + u * P
                        nc.tensor.transpose(xt[:, r, u, :], xw[:, col : col + P], ident[:])
                turned[c].append(xt)

        def copy_x(c):
            g = grp.tile([P, CH * K], BF16, name="g", align_bytes=64)
            gw = g[:].bitcast(F32)
            for j, xt in enumerate(turned[c]):
                nc.scalar.copy(
                    out=gw[:, j * 512 : (j + 1) * 512].rearrange("p (r m u) -> p r m u", r=2, u=2),
                    in_=xt[:].rearrange("p r u m -> p r m u"),
                )
            groups[c] = g

        def quantise_x(c):
            cs = slice(c * CH * P, (c + 1) * CH * P)
            nc.vector.quantize_mx(out=x_codes[:, cs].bitcast(FP8X4), scales=x_scales[:, cs], in_=groups[c][:])

        turn_x(0)
        copy_x(0)

        alpha = const.tile([P, 1], F32, name="alpha")
        nc.vector.tensor_reduce(out=alpha[:], in_=psum_s[:], axis=AX.X, op=ALU.add)
        apos = const.tile([P, P], BF16, name="apos")
        aneg = const.tile([P, P], BF16, name="aneg")
        sc = const.tile([P, 4], F32, name="sc")
        t1r = const.tile([P, 4, N - NV], BF16, name="t1r")
        t2r = const.tile([P, 4, N - NV], BF16, name="t2r")
        t1 = const.tile([P, 4 * NV], BF16, name="t1")
        t2 = const.tile([P, 4 * NV], BF16, name="t2")
        wt = const.tile([P, 4 * N], BF16, name="wt", align_bytes=64)
        w_codes = const.tile([P, N], U32, name="w_codes", align_bytes=64)
        w_scales = const.tile([P, N], U8, name="w_scales", align_bytes=64)

        def above(dst, src):
            nc.vector.tensor_scalar(
                out=dst, in0=src, scalar1=sc[:, 0:1], scalar2=sc[:, 1:2], op0=ALU.is_ge, op1=ALU.mult
            )

        def below(dst, src):
            nc.vector.tensor_scalar(
                out=dst, in0=src, scalar1=sc[:, 2:3], scalar2=sc[:, 3:4], op0=ALU.is_le, op1=ALU.mult
            )

        def quantise_w(h):
            sl = slice(h * 4 * HALF, (h + 1) * 4 * HALF)
            hs = slice(h * HALF, (h + 1) * HALF)
            nc.vector.quantize_mx(out=w_codes[:, hs].bitcast(FP8X4), scales=w_scales[:, hs], in_=wt[:, sl])

        def is_above(dst, src, sign):
            nc.vector.tensor_scalar(
                out=dst, in0=src, scalar1=sign / 0.7, scalar2=alpha[:, 0:1], op0=ALU.mult, op1=ALU.is_ge
            )

        def raw_above(lo, hi):
            is_above(t1r[:, :, lo * P : hi * P], w_tn[:, :, NV + lo * P : NV + hi * P], 1.0)

        def raw_below(lo, hi):
            is_above(t2r[:, :, lo * P : hi * P], w_tn[:, :, NV + lo * P : NV + hi * P], -1.0)

        raw_above(0, 1)
        nc.vector.tensor_scalar(out=apos[:], in0=identb[:], scalar1=alpha[:, 0:1], scalar2=None, op0=ALU.mult)
        raw_below(0, 1)
        nc.vector.tensor_scalar(
            out=aneg[:], in0=identb[:], scalar1=alpha[:, 0:1], scalar2=-1.0, op0=ALU.mult, op1=ALU.mult
        )
        nc.vector.tensor_scalar(out=sc[:], in0=cst[:], scalar1=alpha[:, 0:1], scalar2=None, op0=ALU.mult)
        raw_above(1, 3)
        raw_below(1, 3)
        above(t1[:], wg[:])
        raw_above(3, 5)
        below(t2[:], wg[:])
        raw_below(3, 5)
        nc.vector.tensor_tensor(out=wt[:, 0 : 4 * NV], in0=t1[:], in1=t2[:], op=ALU.add)
        quantise_x(0)
        for c in range((N - NV) // P):
            wp = ps_o.tile([P, 4, P], F32, name="wp", tag="acc")
            for t in range(4):
                for i, (factor, part) in enumerate(((apos, t1r), (aneg, t2r))):
                    nc.tensor.matmul(
                        wp[:, t, :], lhsT=factor[:], rhs=part[:, t, c * P : (c + 1) * P], start=(i == 0), stop=(i == 1)
                    )
            nc.scalar.copy(
                out=wt[:, 4 * (NV + c * P) : 4 * (NV + (c + 1) * P)].rearrange("p (n t) -> p n t", t=4),
                in_=wp[:].rearrange("p t n -> p n t"),
            )
        quantise_w(0)
        quantise_w(1)
        turn_x(1)

        o_tiles = {}
        accs = {}

        def multiply(t, h):
            ts = slice(t * P, (t + 1) * P)
            hs = slice(h * HALF, (h + 1) * HALF)
            acc = ps_o.tile([P, HALF], F32, name="acc")
            nc.tensor.matmul_mx(
                out=acc[:],
                lhsT=x_codes[:, ts].bitcast(FP8X4),
                lhsT_scale=x_scales[:, ts],
                rhs=w_codes[:, hs].bitcast(FP8X4),
                rhs_scale=w_scales[:, hs],
                start=True,
                stop=True,
            )
            accs[t, h] = acc

        def target(j, t, h):
            if j not in o_tiles:
                o_tiles[j] = stage.tile([P, GROUPS[j][1], N], F32, name="o")
            return o_tiles[j][:, t - GROUPS[j][0], h * HALF : (h + 1) * HALF]

        def banks_of(j, scalar):
            t0, nt, s_set = GROUPS[j]
            return [(j, t, h) for t in range(t0, t0 + nt) for h in range(2) if ((t - t0, h) in s_set) == scalar]

        def scalar_banks(j):
            for jj, t, h in banks_of(j, True):
                multiply(t, h)
                o = target(j, t, h)
                nc.scalar.copy(out=o, in_=accs[t, h][:])
                nc.gpsimd.tensor_tensor(out=o, in0=o, in1=b_bc[:, h * HALF : (h + 1) * HALF], op=ALU.add)

        v_list = [bank for j in range(len(GROUPS)) for bank in banks_of(j, False)]

        def vector_bank(i):
            if i + AHEAD < len(v_list):
                multiply(*v_list[i + AHEAD][1:])
            j, t, h = v_list[i]
            nc.vector.tensor_tensor(
                out=target(j, t, h), in0=accs[t, h][:], in1=b_bc[:, h * HALF : (h + 1) * HALF], op=ALU.add
            )

        multiply(0, 0)
        copy_x(1)
        scalar_banks(1)
        for i in range(1, AHEAD):
            multiply(*v_list[i][1:])
        i = 0
        for j in range(len(GROUPS)):
            t0, nt, s_set = GROUPS[j]
            if j in QUANTISE_AT:
                quantise_x(QUANTISE_AT[j])
            for k in range(len(banks_of(j, False))):
                vector_bank(i)
                i += 1
                if j == 0:
                    if k == 0:
                        quantise_x(1)
                    ks = slice(k * HALF, (k + 1) * HALF)
                    nc.sync.dma_start(out=ov[:, t0, ks], in_=o_tiles[j][:, 0, ks])
            if j > 0:
                nc.sync.dma_start(out=ov[:, t0 : t0 + nt, :], in_=o_tiles[j][:])
            for jj in SCALAR_AFTER.get(j, [j + LEAD] if RAMP - LEAD <= j < len(GROUPS) - LEAD else []):
                scalar_banks(jj)
            if j in TURN_AT:
                turn_x(TURN_AT[j])
                copy_x(TURN_AT[j])
